import numpy as np
import ml_dtypes


def mxq(x, axis, fmt="e4m3"):
    dtype, down = {"e4m3": (ml_dtypes.float8_e4m3fn, 7), "e5m2": (ml_dtypes.float8_e5m2, 14)}[fmt]
    v = np.moveaxis(np.asarray(x, np.float32).astype(ml_dtypes.bfloat16).astype(np.float64), axis, -1)
    blocks = v.reshape(v.shape[:-1] + (-1, 32))
    amax = np.abs(blocks).max(-1, keepdims=True)
    byte = np.maximum(np.where(amax > 0, np.frexp(amax)[1] - 1 + 127, 0) - down, 1)
    scale = np.exp2(byte - 127.0)
    codes = (blocks / scale).astype(np.float32).astype(dtype).astype(np.float64)
    return np.moveaxis((codes * scale).reshape(v.shape), -1, axis)


WIDE = False


def mx_kscale(k):
    if not WIDE:
        return np.ones(k)
    levels = np.array([10, -10, 5, -5, 0])
    a = np.random.permutation(np.resize(levels, k // 512 * 4)).reshape(k // 512, 4)
    idx = np.arange(k)
    return np.exp2(a[idx // 512, idx % 128 // 32])


BF16 = ml_dtypes.bfloat16


def bf(x):
    return np.asarray(x, np.float32).astype(BF16)


def f64(x):
    return np.asarray(x).astype(np.float64)


B, IN, HID, CENT = 16384, 128, 512, 256


def setup_inputs():
    t = np.log2(mx_kscale(HID))
    a = t.max() - t
    sigmas = bf(1.0 + 0.1 * np.random.standard_normal(HID))
    c = np.random.standard_normal((HID, IN)) / np.sqrt(IN)
    c = c * np.sqrt(1.0 + a * np.log(2.0) / (f64(sigmas) ** 2 * (c * c).sum(1)))[:, None]
    return {"x": bf(np.random.standard_normal((B, IN)) / np.sqrt(IN)), "centres": bf(c), "sigmas": sigmas,
            "w1": bf(np.random.standard_normal((CENT, HID)) * 6.0 / np.sqrt(HID) * np.exp2(a)),
            "b1": bf(0.2 * np.random.standard_normal(CENT))}


def reference(x, centres, sigmas, w1, b1):
    x2 = np.sum(f64(x) * f64(x), axis=1, keepdims=True)
    c2 = np.sum(f64(centres) * f64(centres), axis=1)[None, :]
    d2 = np.maximum(x2 + c2 - 2.0 * (f64(x) @ f64(centres).T), 0.0)
    phi = np.exp(-d2 * (f64(sigmas) * f64(sigmas))[None, :])
    return np.maximum((mxq(phi, 1, "e4m3") @ mxq(f64(w1), 1, "e4m3").T) + f64(b1), 0.0)

@@ -1,0 +1,180 @@
+import concourse.mybir as mybir
+from concourse.masks import make_identity
+
+F32 = mybir.dt.float32
+BF16 = mybir.dt.bfloat16
+U32 = mybir.dt.uint32
+U8 = mybir.dt.uint8
+FP8X4 = mybir.dt.float8_e4m3fn_x4
+ALU = mybir.AluOpType
+ACT = mybir.ActivationFunctionType
+
+P = 128
+PACK = 4
+ROWS, IN, HID, CENT = 16384, 128, 512, 256
+SUBS = 4
+CHUNK = SUBS * P
+N_CHUNKS = ROWS // CHUNK
+CHUNKS_PER_LOAD = 4
+
+FLOPS = 2 * ROWS * IN * HID + 2 * ROWS * HID * CENT
+
+
+def tile_networkprc_pa_t_kernel(tc, x, centres, sigmas, w1, b1, out):
+    nc = tc.nc
+    assert HID == P * PACK and IN == P and CENT == 2 * P
+
+    x_view = x.rearrange("(q p u) k -> p q (u k)", p=P, u=SUBS)
+    out_view = out.rearrange("(q p u) c -> q p (u c)", p=P, u=SUBS)
+
+    with tc.tile_pool(name="keep", bufs=1) as keep, tc.tile_pool(name="work", bufs=3) as work, tc.psum_pool(
+        name="psum_xt", bufs=1
+    ) as psum_xt, tc.psum_pool(name="psum_dist", bufs=4) as psum_dist, tc.psum_pool(
+        name="psum_acc", bufs=3
+    ) as psum_acc:
+        c_rows = keep.tile([P, PACK, IN], BF16)
+        nc.sync.dma_start(out=c_rows[:], in_=centres.rearrange("(p t) k -> p t k", t=PACK))
+        sig = keep.tile([P, PACK], BF16)
+        nc.sync.dma_start(out=sig[:], in_=sigmas.rearrange("(p t) -> p t", t=PACK))
+        x_all = keep.tile([P, N_CHUNKS, CHUNK], BF16)
+        first = slice(0, CHUNKS_PER_LOAD)
+        nc.sync.dma_start(out=x_all[:, first, :], in_=x_view[:, first, :])
+        w_rows = keep.tile([P, 2, HID], BF16)
+        nc.sync.dma_start(out=w_rows[:], in_=w1.rearrange("(b p) j -> p b j", p=P))
+        bias = keep.tile([P, CENT], BF16)
+        nc.sync.dma_start(out=bias[:], in_=b1.partition_broadcast(P))
+        for q0 in range(CHUNKS_PER_LOAD, N_CHUNKS, CHUNKS_PER_LOAD):
+            later = slice(q0, q0 + CHUNKS_PER_LOAD)
+            nc.sync.dma_start(out=x_all[:, later, :], in_=x_view[:, later, :])
+
+        ident_bf = keep.tile([P, P], BF16)
+        make_identity(nc, ident_bf[:])
+        ident_f32 = keep.tile([P, P], F32)
+        make_identity(nc, ident_f32[:])
+
+        xt_ps = psum_xt.tile([P, SUBS, P], BF16)
+        for t in range(PACK):
+            nc.tensor.transpose(out=xt_ps[:, t, :], in_=c_rows[:, t, :], identity=ident_bf[:])
+        c_cols = keep.tile([P, PACK, P], BF16)
+        nc.vector.tensor_scalar(out=c_cols[:], in0=xt_ps[:], scalar1=-2.0, scalar2=None, op0=ALU.mult)
+
+        c_squares = keep.tile([P, PACK, IN], BF16)
+        c_norm = keep.tile([P, PACK], F32)
+        for t in range(PACK):
+            nc.scalar.activation(
+                out=c_squares[:, t, :], in_=c_rows[:, t, :], func=ACT.Square, accum_out=c_norm[:, t : t + 1]
+            )
+        exp_scale = keep.tile([P, PACK], F32)
+        nc.vector.scalar_tensor_tensor(
+            out=exp_scale[:], in0=sig[:], scalar=-1.0, in1=sig[:], op0=ALU.mult, op1=ALU.mult
+        )
+        exp_bias = keep.tile([P, PACK], F32)
+        nc.vector.tensor_tensor(out=exp_bias[:], in0=exp_scale[:], in1=c_norm[:], op=ALU.mult)
+
+        acc = psum_acc.tile([P, 2, CENT], F32)
+        for b in range(2):
+            words = w_rows[:, b, :].bitcast(F32).rearrange("c (p h) -> c h p", h=2)
+            for h in range(2):
+                nc.tensor.transpose(out=acc[:, h, b * P : (b + 1) * P], in_=words[:, h, :], identity=ident_f32[:])
+        w_grouped = keep.tile([P, CENT * PACK], BF16, align_bytes=64)
+        nc.vector.tensor_copy(
+            out=w_grouped[:].bitcast(F32).rearrange("p (c h) -> p c h", h=2), in_=acc[:].rearrange("p h c -> p c h")
+        )
+        w_codes = keep.tile([P, CENT], U32, align_bytes=64)
+        w_scales = keep.tile([P, CENT], U8, align_bytes=64)
+        nc.vector.quantize_mx(out=w_codes[:].bitcast(FP8X4), scales=w_scales[:], in_=w_grouped[:])
+
+        x_cols, x_norm, phi, phi_grouped, phi_codes, phi_scales, sums = {}, {}, {}, {}, {}, {}, {}
+
+        def transpose_rows(q):
+            squares = work.tile([P, SUBS, IN], BF16)
+            norms = work.tile([P, SUBS], F32)
+            xt_ps = psum_xt.tile([P, SUBS, P], BF16)
+            for u in range(SUBS):
+                rows = x_all[:, q, u * IN : (u + 1) * IN]
+                nc.scalar.activation(out=squares[:, u, :], in_=rows, func=ACT.Square, accum_out=norms[:, u : u + 1])
+                nc.tensor.transpose(out=xt_ps[:, u, :], in_=rows, identity=ident_bf[:])
+            cols = work.tile([P, SUBS, P], BF16)
+            nc.vector.tensor_copy(out=cols[:], in_=xt_ps[:])
+            x_cols[q], x_norm[q] = cols, norms
+
+        def distances_and_exp(q):
+            planes = work.tile([P, PACK, CHUNK], BF16)
+            for t in range(PACK):
+                dist = psum_dist.tile([P, CHUNK], F32)
+                nc.tensor.matmul(
+                    out=dist[:],
+                    lhsT=c_cols[:, t, :],
+                    rhs=x_cols[q][:].rearrange("k u p -> k (u p)"),
+                    start=True,
+                    stop=False,
+                )
+                for u in range(SUBS):
+                    nc.tensor.matmul(
+                        out=dist[:, u * P : (u + 1) * P],
+                        lhsT=x_norm[q][:, u : u + 1].to_broadcast([P, P]),
+                        rhs=ident_f32[:],
+                        is_transpose=True,
+                        start=False,
+                        stop=(u == SUBS - 1),
+                    )
+                nc.scalar.activation(
+                    out=planes[:, t, :],
+                    in_=dist[:],
+                    func=ACT.Exp,
+                    scale=exp_scale[:, t : t + 1],
+                    bias=exp_bias[:, t : t + 1],
+                )
+            phi[q] = planes
+
+        def regroup(q):
+            grouped = work.tile([P, CHUNK * PACK], BF16, align_bytes=64)
+            nc.vector.tensor_scalar(
+                out=grouped[:].rearrange("p (c i t) -> p c t i", i=4, t=PACK),
+                in0=phi[q][:].rearrange("p t (c i) -> p c t i", i=4),
+                scalar1=1.0,
+                scalar2=None,
+                op0=ALU.min,
+            )
+            phi_grouped[q] = grouped
+
+        def quantise(q):
+            codes = work.tile([P, CHUNK], U32, align_bytes=64)
+            scales = work.tile([P, CHUNK], U8, align_bytes=64)
+            nc.vector.quantize_mx(out=codes[:].bitcast(FP8X4), scales=scales[:], in_=phi_grouped[q][:])
+            phi_codes[q], phi_scales[q] = codes, scales
+
+        def project(q):
+            sums[q] = []
+            for half in range(SUBS // 2):
+                acc = psum_acc.tile([P, 2, CENT], F32)
+                for v in range(2):
+                    n_cols = slice((2 * half + v) * P, (2 * half + v + 1) * P)
+                    nc.tensor.matmul_mx(
+                        out=acc[:, v, :],
+                        lhsT=phi_codes[q][:, n_cols].bitcast(FP8X4),
+                        lhsT_scale=phi_scales[q][:, n_cols],
+                        rhs=w_codes[:].bitcast(FP8X4),
+                        rhs_scale=w_scales[:],
+                        start=True,
+                        stop=True,
+                    )
+                sums[q].append(acc)
+
+        def finish(q):
+            result = work.tile([P, SUBS, CENT], F32)
+            for half in range(SUBS // 2):
+                nc.vector.tensor_tensor(
+                    out=result[:, 2 * half : 2 * half + 2, :],
+                    in0=sums[q][half][:],
+                    in1=bias[:].unsqueeze(1).to_broadcast([P, 2, CENT]),
+                    op=ALU.add,
+                )
+            nc.gpsimd.tensor_scalar(out=result[:], in0=result[:], scalar1=0.0, scalar2=0.0, op0=ALU.max, op1=ALU.add)
+            nc.sync.dma_start(out=out_view[q], in_=result[:].rearrange("p u c -> p (u c)"))
+
+        stages = (transpose_rows, distances_and_exp, regroup, quantise, project, finish)
+        for step in range(N_CHUNKS + len(stages) - 1):
+            for lag, stage in enumerate(stages):
+                if 0 <= step - lag < N_CHUNKS:
+                    stage(step - lag)

@@ -84,7 +84,7 @@ def tile_networkprc_pa_t_kernel(tc, x, centres, sigmas, w1, b1, out):
         w_scales = keep.tile([P, CENT], U8, align_bytes=64)
         nc.vector.quantize_mx(out=w_codes[:].bitcast(FP8X4), scales=w_scales[:], in_=w_grouped[:])
 
-        x_cols, x_norm, phi, phi_grouped, phi_codes, phi_scales, sums = {}, {}, {}, {}, {}, {}, {}
+        x_cols, x_norm, phi, phi_grouped, phi_codes, phi_scales, sums, biased = {}, {}, {}, {}, {}, {}, {}, {}
 
         def transpose_rows(q):
             squares = work.tile([P, SUBS, IN], BF16)
@@ -95,7 +95,7 @@ def tile_networkprc_pa_t_kernel(tc, x, centres, sigmas, w1, b1, out):
                 nc.scalar.activation(out=squares[:, u, :], in_=rows, func=ACT.Square, accum_out=norms[:, u : u + 1])
                 nc.tensor.transpose(out=xt_ps[:, u, :], in_=rows, identity=ident_bf[:])
             cols = work.tile([P, SUBS, P], BF16)
-            nc.vector.tensor_copy(out=cols[:], in_=xt_ps[:])
+            nc.scalar.copy(out=cols[:], in_=xt_ps[:])
             x_cols[q], x_norm[q] = cols, norms
 
         def distances_and_exp(q):
@@ -161,7 +161,7 @@ def tile_networkprc_pa_t_kernel(tc, x, centres, sigmas, w1, b1, out):
                     )
                 sums[q].append(acc)
 
-        def finish(q):
+        def add_bias(q):
             result = work.tile([P, SUBS, CENT], F32)
             for half in range(SUBS // 2):
                 nc.vector.tensor_tensor(
@@ -170,10 +170,13 @@ def tile_networkprc_pa_t_kernel(tc, x, centres, sigmas, w1, b1, out):
                     in1=bias[:].unsqueeze(1).to_broadcast([P, 2, CENT]),
                     op=ALU.add,
                 )
-            nc.gpsimd.tensor_scalar(out=result[:], in0=result[:], scalar1=0.0, scalar2=0.0, op0=ALU.max, op1=ALU.add)
-            nc.sync.dma_start(out=out_view[q], in_=result[:].rearrange("p u c -> p (u c)"))
+            biased[q] = result
 
-        stages = (transpose_rows, distances_and_exp, regroup, quantise, project, finish)
+        def relu_and_store(q):
+            nc.vector.tensor_scalar(out=biased[q][:], in0=biased[q][:], scalar1=0.0, scalar2=None, op0=ALU.max)
+            nc.sync.dma_start(out=out_view[q], in_=biased[q][:].rearrange("p u c -> p (u c)"))
+
+        stages = (transpose_rows, distances_and_exp, regroup, quantise, project, add_bias, relu_and_store)
         for step in range(N_CHUNKS + len(stages) - 1):
             for lag, stage in enumerate(stages):
                 if 0 <= step - lag < N_CHUNKS:

@@ -176,8 +176,16 @@ def tile_networkprc_pa_t_kernel(tc, x, centres, sigmas, w1, b1, out):
             nc.vector.tensor_scalar(out=biased[q][:], in0=biased[q][:], scalar1=0.0, scalar2=None, op0=ALU.max)
             nc.sync.dma_start(out=out_view[q], in_=biased[q][:].rearrange("p u c -> p (u c)"))
 
-        stages = (transpose_rows, distances_and_exp, regroup, quantise, project, add_bias, relu_and_store)
-        for step in range(N_CHUNKS + len(stages) - 1):
-            for lag, stage in enumerate(stages):
+        order = (
+            (transpose_rows, 0),
+            (distances_and_exp, 1),
+            (regroup, 2),
+            (quantise, 3),
+            (project, 3),
+            (add_bias, 4),
+            (relu_and_store, 5),
+        )
+        for step in range(N_CHUNKS + 5):
+            for stage, lag in order:
                 if 0 <= step - lag < N_CHUNKS:
                     stage(step - lag)

@@ -16,6 +16,7 @@ SUBS = 4
 CHUNK = SUBS * P
 N_CHUNKS = ROWS // CHUNK
 CHUNKS_PER_LOAD = 4
+VECTOR_ROWS = 384
 
 FLOPS = 2 * ROWS * IN * HID + 2 * ROWS * HID * CENT
 
@@ -127,16 +128,26 @@ def tile_networkprc_pa_t_kernel(tc, x, centres, sigmas, w1, b1, out):
                 )
             phi[q] = planes
 
+        def regroup_on_gpsimd(q):
+            grouped = work.tile([P, CHUNK * PACK], BF16, align_bytes=64, bufs=1)
+            nc.gpsimd.tensor_scalar(
+                out=grouped[:, VECTOR_ROWS * PACK :].rearrange("p (n t) -> p n t", t=PACK),
+                in0=phi[q][:, :, VECTOR_ROWS:].rearrange("p t n -> p n t"),
+                scalar1=1.0,
+                scalar2=0.0,
+                op0=ALU.min,
+                op1=ALU.max,
+            )
+            phi_grouped[q] = grouped
+
         def regroup(q):
-            grouped = work.tile([P, CHUNK * PACK], BF16, align_bytes=64)
             nc.vector.tensor_scalar(
-                out=grouped[:].rearrange("p (c i t) -> p c t i", i=4, t=PACK),
-                in0=phi[q][:].rearrange("p t (c i) -> p c t i", i=4),
+                out=phi_grouped[q][:, : VECTOR_ROWS * PACK].rearrange("p (c i t) -> p c t i", i=4, t=PACK),
+                in0=phi[q][:, :, :VECTOR_ROWS].rearrange("p t (c i) -> p c t i", i=4),
                 scalar1=1.0,
                 scalar2=None,
                 op0=ALU.min,
             )
-            phi_grouped[q] = grouped
 
         def quantise(q):
             codes = work.tile([P, CHUNK], U32, align_bytes=64)
@@ -179,10 +190,11 @@ def tile_networkprc_pa_t_kernel(tc, x, centres, sigmas, w1, b1, out):
         order = (
             (transpose_rows, 0),
             (distances_and_exp, 1),
-            (regroup, 2),
             (quantise, 3),
             (project, 3),
+            (regroup_on_gpsimd, 2),
             (add_bias, 4),
+            (regroup, 2),
             (relu_and_store, 5),
         )
         for step in range(N_CHUNKS + 5):

@@ -101,31 +101,35 @@ def tile_networkprc_pa_t_kernel(tc, x, centres, sigmas, w1, b1, out):
 
         def distances_and_exp(q):
             planes = work.tile([P, PACK, CHUNK], BF16)
-            for t in range(PACK):
-                dist = psum_dist.tile([P, CHUNK], F32)
-                nc.tensor.matmul(
-                    out=dist[:],
-                    lhsT=c_cols[:, t, :],
-                    rhs=x_cols[q][:].rearrange("k u p -> k (u p)"),
-                    start=True,
-                    stop=False,
-                )
-                for u in range(SUBS):
+            for pair in range(PACK // 2):
+                banks = []
+                for t in (2 * pair, 2 * pair + 1):
+                    dist = psum_dist.tile([P, CHUNK], F32)
                     nc.tensor.matmul(
-                        out=dist[:, u * P : (u + 1) * P],
-                        lhsT=x_norm[q][:, u : u + 1].to_broadcast([P, P]),
-                        rhs=ident_f32[:],
-                        is_transpose=True,
-                        start=False,
-                        stop=(u == SUBS - 1),
+                        out=dist[:],
+                        lhsT=c_cols[:, t, :],
+                        rhs=x_cols[q][:].rearrange("k u p -> k (u p)"),
+                        start=True,
+                        stop=False,
                     )
-                nc.scalar.activation(
-                    out=planes[:, t, :],
-                    in_=dist[:],
-                    func=ACT.Exp,
-                    scale=exp_scale[:, t : t + 1],
-                    bias=exp_bias[:, t : t + 1],
-                )
+                    banks.append(dist)
+                for t, dist in zip((2 * pair, 2 * pair + 1), banks):
+                    for u in range(SUBS):
+                        nc.tensor.matmul(
+                            out=dist[:, u * P : (u + 1) * P],
+                            lhsT=x_norm[q][:, u : u + 1].to_broadcast([P, P]),
+                            rhs=ident_f32[:],
+                            is_transpose=True,
+                            start=False,
+                            stop=(u == SUBS - 1),
+                        )
+                    nc.scalar.activation(
+                        out=planes[:, t, :],
+                        in_=dist[:],
+                        func=ACT.Exp,
+                        scale=exp_scale[:, t : t + 1],
+                        bias=exp_bias[:, t : t + 1],
+                    )
             phi[q] = planes
 
         def regroup_on_gpsimd(q):

@@ -8,6 +8,8 @@ U8 = mybir.dt.uint8
 FP8X4 = mybir.dt.float8_e4m3fn_x4
 ALU = mybir.AluOpType
 ACT = mybir.ActivationFunctionType
+AXIS = mybir.AxisListType
+ENGINE = mybir.EngineType
 
 P = 128
 PACK = 4
@@ -15,6 +17,9 @@ ROWS, IN, HID, CENT = 16384, 128, 512, 256
 SUBS = 4
 CHUNK = SUBS * P
 N_CHUNKS = ROWS // CHUNK
+LAST = N_CHUNKS - 1
+ALL = slice(0, CHUNK)
+HALVES = (slice(0, CHUNK // 2), slice(CHUNK // 2, CHUNK))
 CHUNKS_PER_LOAD = 4
 VECTOR_ROWS = 384
 
@@ -33,166 +38,284 @@ def tile_networkprc_pa_t_kernel(tc, x, centres, sigmas, w1, b1, out):
     ) as psum_xt, tc.psum_pool(name="psum_dist", bufs=4) as psum_dist, tc.psum_pool(
         name="psum_acc", bufs=3
     ) as psum_acc:
-        c_rows = keep.tile([P, PACK, IN], BF16)
-        nc.sync.dma_start(out=c_rows[:], in_=centres.rearrange("(p t) k -> p t k", t=PACK))
-        sig = keep.tile([P, PACK], BF16)
-        nc.sync.dma_start(out=sig[:], in_=sigmas.rearrange("(p t) -> p t", t=PACK))
         x_all = keep.tile([P, N_CHUNKS, CHUNK], BF16)
-        first = slice(0, CHUNKS_PER_LOAD)
-        nc.sync.dma_start(out=x_all[:, first, :], in_=x_view[:, first, :])
+        c_rows = keep.tile([P, PACK, IN], BF16)
+        sig = keep.tile([P, PACK], BF16)
         w_rows = keep.tile([P, 2, HID], BF16)
-        nc.sync.dma_start(out=w_rows[:], in_=w1.rearrange("(b p) j -> p b j", p=P))
         bias = keep.tile([P, CENT], BF16)
+
+        def load_chunks(first, end):
+            nc.sync.dma_start(out=x_all[:, first:end, :], in_=x_view[:, first:end, :])
+
+        load_chunks(0, 1)
+        nc.sync.dma_start(out=c_rows[:], in_=centres.rearrange("(p t) k -> p t k", t=PACK))
+        nc.sync.dma_start(out=sig[:], in_=sigmas.rearrange("(p t) -> p t", t=PACK))
+        load_chunks(1, 2)
+        load_chunks(2, CHUNKS_PER_LOAD)
+        nc.sync.dma_start(out=w_rows[:], in_=w1.rearrange("(b p) j -> p b j", p=P))
         nc.sync.dma_start(out=bias[:], in_=b1.partition_broadcast(P))
-        for q0 in range(CHUNKS_PER_LOAD, N_CHUNKS, CHUNKS_PER_LOAD):
-            later = slice(q0, q0 + CHUNKS_PER_LOAD)
-            nc.sync.dma_start(out=x_all[:, later, :], in_=x_view[:, later, :])
+        for q in range(CHUNKS_PER_LOAD, N_CHUNKS, CHUNKS_PER_LOAD):
+            load_chunks(q, q + CHUNKS_PER_LOAD)
 
         ident_bf = keep.tile([P, P], BF16)
         make_identity(nc, ident_bf[:])
         ident_f32 = keep.tile([P, P], F32)
         make_identity(nc, ident_f32[:])
 
-        xt_ps = psum_xt.tile([P, SUBS, P], BF16)
-        for t in range(PACK):
-            nc.tensor.transpose(out=xt_ps[:, t, :], in_=c_rows[:, t, :], identity=ident_bf[:])
-        c_cols = keep.tile([P, PACK, P], BF16)
-        nc.vector.tensor_scalar(out=c_cols[:], in0=xt_ps[:], scalar1=-2.0, scalar2=None, op0=ALU.mult)
-
-        c_squares = keep.tile([P, PACK, IN], BF16)
-        c_norm = keep.tile([P, PACK], F32)
-        for t in range(PACK):
-            nc.scalar.activation(
-                out=c_squares[:, t, :], in_=c_rows[:, t, :], func=ACT.Square, accum_out=c_norm[:, t : t + 1]
-            )
-        exp_scale = keep.tile([P, PACK], F32)
-        nc.vector.scalar_tensor_tensor(
-            out=exp_scale[:], in0=sig[:], scalar=-1.0, in1=sig[:], op0=ALU.mult, op1=ALU.mult
-        )
-        exp_bias = keep.tile([P, PACK], F32)
-        nc.vector.tensor_tensor(out=exp_bias[:], in0=exp_scale[:], in1=c_norm[:], op=ALU.mult)
-
-        acc = psum_acc.tile([P, 2, CENT], F32)
-        for b in range(2):
-            words = w_rows[:, b, :].bitcast(F32).rearrange("c (p h) -> c h p", h=2)
-            for h in range(2):
-                nc.tensor.transpose(out=acc[:, h, b * P : (b + 1) * P], in_=words[:, h, :], identity=ident_f32[:])
-        w_grouped = keep.tile([P, CENT * PACK], BF16, align_bytes=64)
-        nc.vector.tensor_copy(
-            out=w_grouped[:].bitcast(F32).rearrange("p (c h) -> p c h", h=2), in_=acc[:].rearrange("p h c -> p c h")
-        )
-        w_codes = keep.tile([P, CENT], U32, align_bytes=64)
-        w_scales = keep.tile([P, CENT], U8, align_bytes=64)
-        nc.vector.quantize_mx(out=w_codes[:].bitcast(FP8X4), scales=w_scales[:], in_=w_grouped[:])
-
         x_cols, x_norm, phi, phi_grouped, phi_codes, phi_scales, sums, biased = {}, {}, {}, {}, {}, {}, {}, {}
 
-        def transpose_rows(q):
+        def rows_of(q, u):
+            return x_all[:, q, u * IN : (u + 1) * IN]
+
+        def square_rows(q):
             squares = work.tile([P, SUBS, IN], BF16)
             norms = work.tile([P, SUBS], F32)
+            for u in range(SUBS):
+                nc.scalar.activation(
+                    out=squares[:, u, :], in_=rows_of(q, u), func=ACT.Square, accum_out=norms[:, u : u + 1]
+                )
+            x_norm[q] = norms
+
+        def transpose_rows(q):
             xt_ps = psum_xt.tile([P, SUBS, P], BF16)
             for u in range(SUBS):
-                rows = x_all[:, q, u * IN : (u + 1) * IN]
-                nc.scalar.activation(out=squares[:, u, :], in_=rows, func=ACT.Square, accum_out=norms[:, u : u + 1])
-                nc.tensor.transpose(out=xt_ps[:, u, :], in_=rows, identity=ident_bf[:])
+                nc.tensor.transpose(out=xt_ps[:, u, :], in_=rows_of(q, u), identity=ident_bf[:])
             cols = work.tile([P, SUBS, P], BF16)
             nc.scalar.copy(out=cols[:], in_=xt_ps[:])
-            x_cols[q], x_norm[q] = cols, norms
+            x_cols[q] = cols
 
-        def distances_and_exp(q):
-            planes = work.tile([P, PACK, CHUNK], BF16)
-            for pair in range(PACK // 2):
-                banks = []
-                for t in (2 * pair, 2 * pair + 1):
-                    dist = psum_dist.tile([P, CHUNK], F32)
+        def square_and_transpose(q):
+            square_rows(q)
+            transpose_rows(q)
+
+        c_cols = keep.tile([P, PACK, P], BF16)
+        exp_scale = keep.tile([P, PACK], F32)
+        exp_bias = keep.tile([P, PACK], F32)
+
+        def prepare_centres():
+            c_squares = keep.tile([P, PACK, IN], F32)
+            nc.vector.tensor_tensor(out=c_squares[:], in0=c_rows[:], in1=c_rows[:], op=ALU.mult)
+            ct_ps = psum_acc.tile([P, PACK, P], BF16, tag="acc")
+            for t in range(PACK):
+                nc.tensor.transpose(out=ct_ps[:, t, :], in_=c_rows[:, t, :], identity=ident_bf[:])
+            nc.vector.tensor_scalar(out=c_cols[:], in0=ct_ps[:], scalar1=-2.0, scalar2=None, op0=ALU.mult)
+            c_norm = keep.tile([P, PACK], F32)
+            nc.vector.tensor_reduce(out=c_norm[:], in_=c_squares[:], axis=AXIS.X, op=ALU.add)
+            nc.vector.scalar_tensor_tensor(
+                out=exp_scale[:], in0=sig[:], scalar=-1.0, in1=sig[:], op0=ALU.mult, op1=ALU.mult
+            )
+            nc.vector.tensor_tensor(out=exp_bias[:], in0=exp_scale[:], in1=c_norm[:], op=ALU.mult)
+
+        w_codes = keep.tile([P, CENT], U32, align_bytes=64)
+        w_scales = keep.tile([P, CENT], U8, align_bytes=64)
+
+        def quantise_weights():
+            acc = psum_acc.tile([P, 2, CENT], F32)
+            for b in range(2):
+                words = w_rows[:, b, :].bitcast(F32).rearrange("c (p h) -> c h p", h=2)
+                for h in range(2):
+                    nc.tensor.transpose(out=acc[:, h, b * P : (b + 1) * P], in_=words[:, h, :], identity=ident_f32[:])
+            w_grouped = keep.tile([P, CENT * PACK], BF16, align_bytes=64)
+            nc.vector.tensor_copy(
+                out=w_grouped[:].bitcast(F32).rearrange("p (c h) -> p c h", h=2), in_=acc[:].rearrange("p h c -> p c h")
+            )
+            nc.vector.quantize_mx(out=w_codes[:].bitcast(FP8X4), scales=w_scales[:], in_=w_grouped[:])
+
+        def distances_with_norms(q, pair):
+            banks = []
+            for t in (2 * pair, 2 * pair + 1):
+                dist = psum_dist.tile([P, CHUNK], F32)
+                nc.tensor.matmul(
+                    out=dist[:],
+                    lhsT=c_cols[:, t, :],
+                    rhs=x_cols[q][:].rearrange("k u p -> k (u p)"),
+                    start=True,
+                    stop=False,
+                )
+                banks.append((t, dist))
+            for t, dist in banks:
+                for u in range(SUBS):
                     nc.tensor.matmul(
-                        out=dist[:],
-                        lhsT=c_cols[:, t, :],
-                        rhs=x_cols[q][:].rearrange("k u p -> k (u p)"),
-                        start=True,
-                        stop=False,
+                        out=dist[:, u * P : (u + 1) * P],
+                        lhsT=x_norm[q][:, u : u + 1].to_broadcast([P, P]),
+                        rhs=ident_f32[:],
+                        is_transpose=True,
+                        start=False,
+                        stop=(u == SUBS - 1),
                     )
-                    banks.append(dist)
-                for t, dist in zip((2 * pair, 2 * pair + 1), banks):
-                    for u in range(SUBS):
-                        nc.tensor.matmul(
-                            out=dist[:, u * P : (u + 1) * P],
-                            lhsT=x_norm[q][:, u : u + 1].to_broadcast([P, P]),
-                            rhs=ident_f32[:],
-                            is_transpose=True,
-                            start=False,
-                            stop=(u == SUBS - 1),
-                        )
-                    nc.scalar.activation(
-                        out=planes[:, t, :],
-                        in_=dist[:],
-                        func=ACT.Exp,
-                        scale=exp_scale[:, t : t + 1],
-                        bias=exp_bias[:, t : t + 1],
-                    )
+            return banks
+
+        def exp(q, t, dist, rows=ALL):
+            nc.scalar.activation(
+                out=phi[q][:, t, rows],
+                in_=dist[:, rows],
+                func=ACT.Exp,
+                scale=exp_scale[:, t : t + 1],
+                bias=exp_bias[:, t : t + 1],
+            )
+
+        def new_phi(q):
+            planes = work.tile([P, PACK, CHUNK], BF16)
             phi[q] = planes
 
-        def regroup_on_gpsimd(q):
+        def distances_and_exp_pair(q, pair):
+            for t, dist in distances_with_norms(q, pair):
+                exp(q, t, dist)
+
+        def distances_and_exp(q):
+            new_phi(q)
+            for pair in range(PACK // 2):
+                distances_and_exp_pair(q, pair)
+
+        def new_grouped(q):
             grouped = work.tile([P, CHUNK * PACK], BF16, align_bytes=64, bufs=1)
+            phi_grouped[q] = grouped
+
+        def regroup_on_gpsimd(q):
+            new_grouped(q)
             nc.gpsimd.tensor_scalar(
-                out=grouped[:, VECTOR_ROWS * PACK :].rearrange("p (n t) -> p n t", t=PACK),
+                out=phi_grouped[q][:, VECTOR_ROWS * PACK :].rearrange("p (n t) -> p n t", t=PACK),
                 in0=phi[q][:, :, VECTOR_ROWS:].rearrange("p t n -> p n t"),
                 scalar1=1.0,
                 scalar2=0.0,
                 op0=ALU.min,
                 op1=ALU.max,
             )
-            phi_grouped[q] = grouped
 
-        def regroup(q):
+        def regroup(q, rows=slice(0, VECTOR_ROWS)):
+            words = slice(rows.start * PACK, rows.stop * PACK)
             nc.vector.tensor_scalar(
-                out=phi_grouped[q][:, : VECTOR_ROWS * PACK].rearrange("p (c i t) -> p c t i", i=4, t=PACK),
-                in0=phi[q][:, :, :VECTOR_ROWS].rearrange("p t (c i) -> p c t i", i=4),
+                out=phi_grouped[q][:, words].rearrange("p (c i t) -> p c t i", i=4, t=PACK),
+                in0=phi[q][:, :, rows].rearrange("p t (c i) -> p c t i", i=4),
                 scalar1=1.0,
                 scalar2=None,
                 op0=ALU.min,
             )
 
-        def quantise(q):
-            codes = work.tile([P, CHUNK], U32, align_bytes=64)
-            scales = work.tile([P, CHUNK], U8, align_bytes=64)
-            nc.vector.quantize_mx(out=codes[:].bitcast(FP8X4), scales=scales[:], in_=phi_grouped[q][:])
-            phi_codes[q], phi_scales[q] = codes, scales
+        def quantise(q, rows=ALL):
+            if rows.start == 0:
+                codes = work.tile([P, CHUNK], U32, align_bytes=64)
+                scales = work.tile([P, CHUNK], U8, align_bytes=64)
+                phi_codes[q], phi_scales[q] = codes, scales
+            nc.vector.quantize_mx(
+                out=phi_codes[q][:, rows].bitcast(FP8X4),
+                scales=phi_scales[q][:, rows],
+                in_=phi_grouped[q][:, rows.start * PACK : rows.stop * PACK],
+            )
+
+        def project_half(q, half):
+            acc = psum_acc.tile([P, 2, CENT], F32)
+            for v in range(2):
+                n_cols = slice((2 * half + v) * P, (2 * half + v + 1) * P)
+                nc.tensor.matmul_mx(
+                    out=acc[:, v, :],
+                    lhsT=phi_codes[q][:, n_cols].bitcast(FP8X4),
+                    lhsT_scale=phi_scales[q][:, n_cols],
+                    rhs=w_codes[:].bitcast(FP8X4),
+                    rhs_scale=w_scales[:],
+                    start=True,
+                    stop=True,
+                )
+            sums[q, half] = acc
 
         def project(q):
-            sums[q] = []
-            for half in range(SUBS // 2):
-                acc = psum_acc.tile([P, 2, CENT], F32)
-                for v in range(2):
-                    n_cols = slice((2 * half + v) * P, (2 * half + v + 1) * P)
-                    nc.tensor.matmul_mx(
-                        out=acc[:, v, :],
-                        lhsT=phi_codes[q][:, n_cols].bitcast(FP8X4),
-                        lhsT_scale=phi_scales[q][:, n_cols],
-                        rhs=w_codes[:].bitcast(FP8X4),
-                        rhs_scale=w_scales[:],
-                        start=True,
-                        stop=True,
-                    )
-                sums[q].append(acc)
+            for half in range(2):
+                project_half(q, half)
+
+        def add_bias_half(q, half):
+            if half == 0:
+                result = work.tile([P, SUBS, CENT], F32)
+                biased[q] = result
+            nc.vector.tensor_tensor(
+                out=biased[q][:, 2 * half : 2 * half + 2, :],
+                in0=sums[q, half][:],
+                in1=bias[:].unsqueeze(1).to_broadcast([P, 2, CENT]),
+                op=ALU.add,
+            )
 
         def add_bias(q):
-            result = work.tile([P, SUBS, CENT], F32)
-            for half in range(SUBS // 2):
-                nc.vector.tensor_tensor(
-                    out=result[:, 2 * half : 2 * half + 2, :],
-                    in0=sums[q][half][:],
-                    in1=bias[:].unsqueeze(1).to_broadcast([P, 2, CENT]),
-                    op=ALU.add,
-                )
-            biased[q] = result
+            for half in range(2):
+                add_bias_half(q, half)
+
+        def relu(tile):
+            nc.vector.tensor_scalar(out=tile, in0=tile, scalar1=0.0, scalar2=None, op0=ALU.max)
+
+        def relu_on_scalar(tile):
+            nc.scalar.activation(out=tile, in_=tile, func=ACT.Relu)
+
+        def store(q, subs=slice(0, SUBS)):
+            nc.sync.dma_start(
+                out=out_view[q][:, subs.start * CENT : subs.stop * CENT],
+                in_=biased[q][:, subs, :].rearrange("p u c -> p (u c)"),
+            )
 
         def relu_and_store(q):
-            nc.vector.tensor_scalar(out=biased[q][:], in0=biased[q][:], scalar1=0.0, scalar2=None, op0=ALU.max)
-            nc.sync.dma_start(out=out_view[q], in_=biased[q][:].rearrange("p u c -> p (u c)"))
+            relu(biased[q][:])
+            store(q)
+
+        def relu_on_scalar_and_store(q):
+            relu_on_scalar(biased[q][:])
+            store(q)
+
+        def warm_up():
+            zeros = keep.tile([P, P], BF16)
+            nc.vector.memset(zeros[:], 0.0)
+            acc = psum_acc.tile([P, CHUNK], F32)
+            for i in range(12):
+                nc.tensor.matmul(out=acc[:, 0:P], lhsT=zeros[:], rhs=zeros[:], start=True, stop=True)
+
+        def start():
+            with tc.manual_schedule(engines={ENGINE.PE, ENGINE.Activation, ENGINE.DVE}):
+                warm_up()
+                square_rows(0)
+                transpose_rows(0)
+                prepare_centres()
+                square_rows(1)
+                new_phi(0)
+                distances_and_exp_pair(0, 0)
+                transpose_rows(1)
+                distances_and_exp_pair(0, 1)
+                quantise_weights()
+
+        def finish():
+            with tc.manual_schedule(engines={ENGINE.PE, ENGINE.Activation, ENGINE.DVE}):
+                new_phi(LAST)
+                banks = distances_with_norms(LAST, 0)
+                quantise(LAST - 2)
+                project(LAST - 2)
+                banks = banks + distances_with_norms(LAST, 1)
+                for rows in HALVES:
+                    for t, dist in banks:
+                        exp(LAST, t, dist, rows)
+                regroup_on_gpsimd(LAST - 1)
+                add_bias(LAST - 3)
+                relu_and_store(LAST - 4)
+                add_bias_half(LAST - 2, 0)
+                regroup(LAST - 1)
+                add_bias_half(LAST - 2, 1)
+                quantise(LAST - 1)
+                project(LAST - 1)
+                relu_on_scalar_and_store(LAST - 3)
+                relu_on_scalar_and_store(LAST - 2)
+                new_grouped(LAST)
+                regroup(LAST, HALVES[0])
+                add_bias_half(LAST - 1, 0)
+                quantise(LAST, HALVES[0])
+                project_half(LAST, 0)
+                regroup(LAST, HALVES[1])
+                add_bias_half(LAST - 1, 1)
+                relu_on_scalar_and_store(LAST - 1)
+                quantise(LAST, HALVES[1])
+                project_half(LAST, 1)
+                add_bias_half(LAST, 0)
+                relu_on_scalar(biased[LAST][:, 0:2, :])
+                store(LAST, slice(0, 2))
+                add_bias_half(LAST, 1)
+                relu(biased[LAST][:, 2:SUBS, :])
+                store(LAST, slice(2, SUBS))
 
         order = (
-            (transpose_rows, 0),
+            (square_and_transpose, 0),
             (distances_and_exp, 1),
             (quantise, 3),
             (project, 3),
@@ -201,7 +324,9 @@ def tile_networkprc_pa_t_kernel(tc, x, centres, sigmas, w1, b1, out):
             (regroup, 2),
             (relu_and_store, 5),
         )
-        for step in range(N_CHUNKS + 5):
+        start()
+        for step in range(2, N_CHUNKS):
             for stage, lag in order:
-                if 0 <= step - lag < N_CHUNKS:
+                if step >= lag:
                     stage(step - lag)
+        finish()

@@ -21,7 +21,9 @@ LAST = N_CHUNKS - 1
 ALL = slice(0, CHUNK)
 HALVES = (slice(0, CHUNK // 2), slice(CHUNK // 2, CHUNK))
 CHUNKS_PER_LOAD = 4
-VECTOR_ROWS = 384
+VECTOR_COPIES = 3
+GPSIMD_FROM = 384
+VECTOR_ROWS = GPSIMD_FROM + 8
 
 FLOPS = 2 * ROWS * IN * HID + 2 * ROWS * HID * CENT
 
@@ -62,7 +64,7 @@ def tile_networkprc_pa_t_kernel(tc, x, centres, sigmas, w1, b1, out):
         ident_f32 = keep.tile([P, P], F32)
         make_identity(nc, ident_f32[:])
 
-        x_cols, x_norm, phi, phi_grouped, phi_codes, phi_scales, sums, biased = {}, {}, {}, {}, {}, {}, {}, {}
+        x_turned, x_cols, x_norm, phi, phi_grouped, phi_codes, phi_scales, sums, biased = {}, {}, {}, {}, {}, {}, {}, {}, {}
 
         def rows_of(q, u):
             return x_all[:, q, u * IN : (u + 1) * IN]
@@ -81,12 +83,21 @@ def tile_networkprc_pa_t_kernel(tc, x, centres, sigmas, w1, b1, out):
             for u in range(SUBS):
                 nc.tensor.transpose(out=xt_ps[:, u, :], in_=rows_of(q, u), identity=ident_bf[:])
             cols = work.tile([P, SUBS, P], BF16)
-            nc.scalar.copy(out=cols[:], in_=xt_ps[:])
             x_cols[q] = cols
+            x_turned[q] = xt_ps
+
+        def copy_on_scalar(q):
+            nc.scalar.copy(out=x_cols[q][:], in_=x_turned[q][:])
+
+        def copy_on_vector(q):
+            if q % VECTOR_COPIES == 0:
+                nc.vector.tensor_copy(out=x_cols[q][:], in_=x_turned[q][:])
 
         def square_and_transpose(q):
             square_rows(q)
             transpose_rows(q)
+            if q % VECTOR_COPIES != 0:
+                copy_on_scalar(q)
 
         c_cols = keep.tile([P, PACK, P], BF16)
         exp_scale = keep.tile([P, PACK], F32)
@@ -162,20 +173,14 @@ def tile_networkprc_pa_t_kernel(tc, x, centres, sigmas, w1, b1, out):
             for t, dist in distances_with_norms(q, pair):
                 exp(q, t, dist)
 
-        def distances_and_exp(q):
-            new_phi(q)
-            for pair in range(PACK // 2):
-                distances_and_exp_pair(q, pair)
-
         def new_grouped(q):
-            grouped = work.tile([P, CHUNK * PACK], BF16, align_bytes=64, bufs=1)
+            grouped = work.tile([P, CHUNK * PACK], BF16, align_bytes=64)
             phi_grouped[q] = grouped
 
         def regroup_on_gpsimd(q):
-            new_grouped(q)
             nc.gpsimd.tensor_scalar(
-                out=phi_grouped[q][:, VECTOR_ROWS * PACK :].rearrange("p (n t) -> p n t", t=PACK),
-                in0=phi[q][:, :, VECTOR_ROWS:].rearrange("p t n -> p n t"),
+                out=phi_grouped[q][:, GPSIMD_FROM * PACK :].rearrange("p (n t) -> p n t", t=PACK),
+                in0=phi[q][:, :, GPSIMD_FROM:].rearrange("p t n -> p n t"),
                 scalar1=1.0,
                 scalar2=0.0,
                 op0=ALU.min,
@@ -183,6 +188,8 @@ def tile_networkprc_pa_t_kernel(tc, x, centres, sigmas, w1, b1, out):
             )
 
         def regroup(q, rows=slice(0, VECTOR_ROWS)):
+            if rows.start == 0:
+                new_grouped(q)
             words = slice(rows.start * PACK, rows.stop * PACK)
             nc.vector.tensor_scalar(
                 out=phi_grouped[q][:, words].rearrange("p (c i t) -> p c t i", i=4, t=PACK),
@@ -224,7 +231,7 @@ def tile_networkprc_pa_t_kernel(tc, x, centres, sigmas, w1, b1, out):
 
         def add_bias_half(q, half):
             if half == 0:
-                result = work.tile([P, SUBS, CENT], F32)
+                result = work.tile([P, SUBS, CENT], F32, bufs=6)
                 biased[q] = result
             nc.vector.tensor_tensor(
                 out=biased[q][:, 2 * half : 2 * half + 2, :],
@@ -269,35 +276,39 @@ def tile_networkprc_pa_t_kernel(tc, x, centres, sigmas, w1, b1, out):
                 warm_up()
                 square_rows(0)
                 transpose_rows(0)
+                copy_on_scalar(0)
                 prepare_centres()
                 square_rows(1)
                 new_phi(0)
                 distances_and_exp_pair(0, 0)
                 transpose_rows(1)
+                copy_on_scalar(1)
                 distances_and_exp_pair(0, 1)
                 quantise_weights()
+
+        def distances_and_exp(q):
+            new_phi(q)
+            for pair in range(PACK // 2):
+                distances_and_exp_pair(q, pair)
 
         def finish():
             with tc.manual_schedule(engines={ENGINE.PE, ENGINE.Activation, ENGINE.DVE}):
                 new_phi(LAST)
                 banks = distances_with_norms(LAST, 0)
-                quantise(LAST - 2)
                 project(LAST - 2)
                 banks = banks + distances_with_norms(LAST, 1)
                 for rows in HALVES:
                     for t, dist in banks:
                         exp(LAST, t, dist, rows)
-                regroup_on_gpsimd(LAST - 1)
                 add_bias(LAST - 3)
-                relu_and_store(LAST - 4)
-                add_bias_half(LAST - 2, 0)
+                relu_on_scalar_and_store(LAST - 4)
                 regroup(LAST - 1)
-                add_bias_half(LAST - 2, 1)
+                regroup_on_gpsimd(LAST - 1)
+                relu_on_scalar_and_store(LAST - 3)
+                add_bias(LAST - 2)
+                relu_on_scalar_and_store(LAST - 2)
                 quantise(LAST - 1)
                 project(LAST - 1)
-                relu_on_scalar_and_store(LAST - 3)
-                relu_on_scalar_and_store(LAST - 2)
-                new_grouped(LAST)
                 regroup(LAST, HALVES[0])
                 add_bias_half(LAST - 1, 0)
                 quantise(LAST, HALVES[0])
@@ -317,16 +328,18 @@ def tile_networkprc_pa_t_kernel(tc, x, centres, sigmas, w1, b1, out):
         order = (
             (square_and_transpose, 0),
             (distances_and_exp, 1),
-            (quantise, 3),
             (project, 3),
+            (regroup, 2),
             (regroup_on_gpsimd, 2),
             (add_bias, 4),
-            (regroup, 2),
+            (copy_on_vector, 0),
             (relu_and_store, 5),
+            (quantise, 2),
         )
         start()
-        for step in range(2, N_CHUNKS):
-            for stage, lag in order:
-                if step >= lag:
-                    stage(step - lag)
+        with tc.manual_schedule(engines={ENGINE.DVE}):
+            for step in range(2, N_CHUNKS):
+                for stage, lag in order:
+                    if step >= lag:
+                        stage(step - lag)
         finish()

@@ -20,8 +20,9 @@ N_CHUNKS = ROWS // CHUNK
 LAST = N_CHUNKS - 1
 ALL = slice(0, CHUNK)
 HALVES = (slice(0, CHUNK // 2), slice(CHUNK // 2, CHUNK))
+PAIRS = ((0, 1), (2, 3))
 CHUNKS_PER_LOAD = 4
-VECTOR_COPIES = 3
+COPIED_ON_VECTOR = range(4, N_CHUNKS, 6)
 GPSIMD_FROM = 384
 VECTOR_ROWS = GPSIMD_FROM + 8
 
@@ -78,26 +79,31 @@ def tile_networkprc_pa_t_kernel(tc, x, centres, sigmas, w1, b1, out):
                 )
             x_norm[q] = norms
 
-        def transpose_rows(q):
-            xt_ps = psum_xt.tile([P, SUBS, P], BF16)
-            for u in range(SUBS):
-                nc.tensor.transpose(out=xt_ps[:, u, :], in_=rows_of(q, u), identity=ident_bf[:])
-            cols = work.tile([P, SUBS, P], BF16)
-            x_cols[q] = cols
-            x_turned[q] = xt_ps
+        def transpose_rows(q, count=2):
+            xt_ps = psum_xt.tile([P, count, SUBS, P], BF16)
+            cols = work.tile([P, count, SUBS, P], BF16)
+            for c in range(count):
+                for u in range(SUBS):
+                    nc.tensor.transpose(out=xt_ps[:, c, u, :], in_=rows_of(q + c, u), identity=ident_bf[:])
+                x_cols[q + c] = cols[:, c, :, :]
+            x_turned[q] = (cols, xt_ps)
 
         def copy_on_scalar(q):
-            nc.scalar.copy(out=x_cols[q][:], in_=x_turned[q][:])
+            cols, xt_ps = x_turned[q]
+            nc.scalar.copy(out=cols[:], in_=xt_ps[:])
 
         def copy_on_vector(q):
-            if q % VECTOR_COPIES == 0:
-                nc.vector.tensor_copy(out=x_cols[q][:], in_=x_turned[q][:])
+            if q in COPIED_ON_VECTOR:
+                cols, xt_ps = x_turned[q]
+                nc.vector.tensor_copy(out=cols[:], in_=xt_ps[:])
 
         def square_and_transpose(q):
-            square_rows(q)
-            transpose_rows(q)
-            if q % VECTOR_COPIES != 0:
-                copy_on_scalar(q)
+            if q not in x_norm:
+                square_rows(q)
+            if q % 2 == 0:
+                transpose_rows(q)
+                if q not in COPIED_ON_VECTOR:
+                    copy_on_scalar(q)
 
         c_cols = keep.tile([P, PACK, P], BF16)
         exp_scale = keep.tile([P, PACK], F32)
@@ -132,14 +138,14 @@ def tile_networkprc_pa_t_kernel(tc, x, centres, sigmas, w1, b1, out):
             )
             nc.vector.quantize_mx(out=w_codes[:].bitcast(FP8X4), scales=w_scales[:], in_=w_grouped[:])
 
-        def distances_with_norms(q, pair):
+        def distances_with_norms(q, planes):
             banks = []
-            for t in (2 * pair, 2 * pair + 1):
+            for t in planes:
                 dist = psum_dist.tile([P, CHUNK], F32)
                 nc.tensor.matmul(
                     out=dist[:],
                     lhsT=c_cols[:, t, :],
-                    rhs=x_cols[q][:].rearrange("k u p -> k (u p)"),
+                    rhs=x_cols[q].rearrange("k u p -> k (u p)"),
                     start=True,
                     stop=False,
                 )
@@ -169,8 +175,8 @@ def tile_networkprc_pa_t_kernel(tc, x, centres, sigmas, w1, b1, out):
             planes = work.tile([P, PACK, CHUNK], BF16)
             phi[q] = planes
 
-        def distances_and_exp_pair(q, pair):
-            for t, dist in distances_with_norms(q, pair):
+        def exp_of_planes(q, planes):
+            for t, dist in distances_with_norms(q, planes):
                 exp(q, t, dist)
 
         def new_grouped(q):
@@ -275,28 +281,29 @@ def tile_networkprc_pa_t_kernel(tc, x, centres, sigmas, w1, b1, out):
             with tc.manual_schedule(engines={ENGINE.PE, ENGINE.Activation, ENGINE.DVE}):
                 warm_up()
                 square_rows(0)
-                transpose_rows(0)
+                transpose_rows(0, 1)
                 copy_on_scalar(0)
                 prepare_centres()
                 square_rows(1)
+                square_rows(2)
                 new_phi(0)
-                distances_and_exp_pair(0, 0)
-                transpose_rows(1)
+                exp_of_planes(0, (0,))
+                exp_of_planes(0, (1,))
+                transpose_rows(1, 1)
                 copy_on_scalar(1)
-                distances_and_exp_pair(0, 1)
+                exp_of_planes(0, PAIRS[1])
                 quantise_weights()
 
         def distances_and_exp(q):
             new_phi(q)
-            for pair in range(PACK // 2):
-                distances_and_exp_pair(q, pair)
+            for pair in PAIRS:
+                exp_of_planes(q, pair)
 
         def finish():
             with tc.manual_schedule(engines={ENGINE.PE, ENGINE.Activation, ENGINE.DVE}):
                 new_phi(LAST)
-                banks = distances_with_norms(LAST, 0)
+                banks = distances_with_norms(LAST, PAIRS[0]) + distances_with_norms(LAST, PAIRS[1])
                 project(LAST - 2)
-                banks = banks + distances_with_norms(LAST, 1)
                 for rows in HALVES:
                     for t, dist in banks:
                         exp(LAST, t, dist, rows)
@@ -337,7 +344,7 @@ def tile_networkprc_pa_t_kernel(tc, x, centres, sigmas, w1, b1, out):
             (quantise, 2),
         )
         start()
-        with tc.manual_schedule(engines={ENGINE.DVE}):
+        with tc.manual_schedule(engines={ENGINE.PE, ENGINE.Activation, ENGINE.DVE}):
             for step in range(2, N_CHUNKS):
                 for stage, lag in order:
                     if step >= lag:

@@ -22,7 +22,7 @@ ALL = slice(0, CHUNK)
 HALVES = (slice(0, CHUNK // 2), slice(CHUNK // 2, CHUNK))
 PAIRS = ((0, 1), (2, 3))
 CHUNKS_PER_LOAD = 4
-COPIED_ON_VECTOR = range(4, N_CHUNKS, 6)
+VECTOR_COPIES = 3
 GPSIMD_FROM = 384
 VECTOR_ROWS = GPSIMD_FROM + 8
 
@@ -79,31 +79,27 @@ def tile_networkprc_pa_t_kernel(tc, x, centres, sigmas, w1, b1, out):
                 )
             x_norm[q] = norms
 
-        def transpose_rows(q, count=2):
-            xt_ps = psum_xt.tile([P, count, SUBS, P], BF16)
-            cols = work.tile([P, count, SUBS, P], BF16)
-            for c in range(count):
-                for u in range(SUBS):
-                    nc.tensor.transpose(out=xt_ps[:, c, u, :], in_=rows_of(q + c, u), identity=ident_bf[:])
-                x_cols[q + c] = cols[:, c, :, :]
-            x_turned[q] = (cols, xt_ps)
+        def transpose_rows(q):
+            xt_ps = psum_xt.tile([P, SUBS, P], BF16)
+            for u in range(SUBS):
+                nc.tensor.transpose(out=xt_ps[:, u, :], in_=rows_of(q, u), identity=ident_bf[:])
+            cols = work.tile([P, SUBS, P], BF16)
+            x_cols[q] = cols
+            x_turned[q] = xt_ps
 
         def copy_on_scalar(q):
-            cols, xt_ps = x_turned[q]
-            nc.scalar.copy(out=cols[:], in_=xt_ps[:])
+            nc.scalar.copy(out=x_cols[q][:], in_=x_turned[q][:])
 
         def copy_on_vector(q):
-            if q in COPIED_ON_VECTOR:
-                cols, xt_ps = x_turned[q]
-                nc.vector.tensor_copy(out=cols[:], in_=xt_ps[:])
+            if q % VECTOR_COPIES == 0:
+                nc.vector.tensor_copy(out=x_cols[q][:], in_=x_turned[q][:])
 
         def square_and_transpose(q):
             if q not in x_norm:
                 square_rows(q)
-            if q % 2 == 0:
-                transpose_rows(q)
-                if q not in COPIED_ON_VECTOR:
-                    copy_on_scalar(q)
+            transpose_rows(q)
+            if q % VECTOR_COPIES != 0:
+                copy_on_scalar(q)
 
         c_cols = keep.tile([P, PACK, P], BF16)
         exp_scale = keep.tile([P, PACK], F32)
@@ -145,7 +141,7 @@ def tile_networkprc_pa_t_kernel(tc, x, centres, sigmas, w1, b1, out):
                 nc.tensor.matmul(
                     out=dist[:],
                     lhsT=c_cols[:, t, :],
-                    rhs=x_cols[q].rearrange("k u p -> k (u p)"),
+                    rhs=x_cols[q][:].rearrange("k u p -> k (u p)"),
                     start=True,
                     stop=False,
                 )
@@ -198,8 +194,8 @@ def tile_networkprc_pa_t_kernel(tc, x, centres, sigmas, w1, b1, out):
                 new_grouped(q)
             words = slice(rows.start * PACK, rows.stop * PACK)
             nc.vector.tensor_scalar(
-                out=phi_grouped[q][:, words].rearrange("p (c i t) -> p c t i", i=4, t=PACK),
-                in0=phi[q][:, :, rows].rearrange("p t (c i) -> p c t i", i=4),
+                out=phi_grouped[q][:, words].rearrange("p (c i t) -> p c t i", i=2, t=PACK),
+                in0=phi[q][:, :, rows].rearrange("p t (c i) -> p c t i", i=2),
                 scalar1=1.0,
                 scalar2=None,
                 op0=ALU.min,
@@ -281,7 +277,7 @@ def tile_networkprc_pa_t_kernel(tc, x, centres, sigmas, w1, b1, out):
             with tc.manual_schedule(engines={ENGINE.PE, ENGINE.Activation, ENGINE.DVE}):
                 warm_up()
                 square_rows(0)
-                transpose_rows(0, 1)
+                transpose_rows(0)
                 copy_on_scalar(0)
                 prepare_centres()
                 square_rows(1)
@@ -289,7 +285,7 @@ def tile_networkprc_pa_t_kernel(tc, x, centres, sigmas, w1, b1, out):
                 new_phi(0)
                 exp_of_planes(0, (0,))
                 exp_of_planes(0, (1,))
-                transpose_rows(1, 1)
+                transpose_rows(1)
                 copy_on_scalar(1)
                 exp_of_planes(0, PAIRS[1])
                 quantise_weights()

@@ -288,12 +288,16 @@ def tile_networkprc_pa_t_kernel(tc, x, centres, sigmas, w1, b1, out):
                 transpose_rows(1)
                 copy_on_scalar(1)
                 exp_of_planes(0, PAIRS[1])
-                quantise_weights()
 
         def distances_and_exp(q):
             new_phi(q)
             for pair in PAIRS:
                 exp_of_planes(q, pair)
+
+        def add_bias_sub(q, sub):
+            nc.vector.tensor_tensor(
+                out=biased[q][:, sub, :], in0=sums[q, sub // 2][:, sub % 2, :], in1=bias[:], op=ALU.add
+            )
 
         def finish():
             with tc.manual_schedule(engines={ENGINE.PE, ENGINE.Activation, ENGINE.DVE}):
@@ -303,20 +307,21 @@ def tile_networkprc_pa_t_kernel(tc, x, centres, sigmas, w1, b1, out):
                 for rows in HALVES:
                     for t, dist in banks:
                         exp(LAST, t, dist, rows)
-                add_bias(LAST - 3)
-                relu_on_scalar_and_store(LAST - 4)
                 regroup(LAST - 1)
                 regroup_on_gpsimd(LAST - 1)
+                add_bias(LAST - 3)
+                relu_on_scalar_and_store(LAST - 4)
                 relu_on_scalar_and_store(LAST - 3)
-                add_bias(LAST - 2)
-                relu_on_scalar_and_store(LAST - 2)
                 quantise(LAST - 1)
                 project(LAST - 1)
+                add_bias(LAST - 2)
+                relu_on_scalar_and_store(LAST - 2)
                 regroup(LAST, HALVES[0])
+                regroup_on_gpsimd(LAST)
                 add_bias_half(LAST - 1, 0)
                 quantise(LAST, HALVES[0])
                 project_half(LAST, 0)
-                regroup(LAST, HALVES[1])
+                regroup(LAST, slice(HALVES[1].start, GPSIMD_FROM))
                 add_bias_half(LAST - 1, 1)
                 relu_on_scalar_and_store(LAST - 1)
                 quantise(LAST, HALVES[1])
@@ -324,18 +329,20 @@ def tile_networkprc_pa_t_kernel(tc, x, centres, sigmas, w1, b1, out):
                 add_bias_half(LAST, 0)
                 relu_on_scalar(biased[LAST][:, 0:2, :])
                 store(LAST, slice(0, 2))
-                add_bias_half(LAST, 1)
-                relu(biased[LAST][:, 2:SUBS, :])
-                store(LAST, slice(2, SUBS))
+                for sub in (2, 3):
+                    add_bias_sub(LAST, sub)
+                for sub in (2, 3):
+                    relu(biased[LAST][:, sub, :])
+                    store(LAST, slice(sub, sub + 1))
 
         order = (
             (square_and_transpose, 0),
             (distances_and_exp, 1),
             (project, 3),
+            (copy_on_vector, 0),
             (regroup, 2),
             (regroup_on_gpsimd, 2),
             (add_bias, 4),
-            (copy_on_vector, 0),
             (relu_and_store, 5),
             (quantise, 2),
         )
@@ -345,4 +352,6 @@ def tile_networkprc_pa_t_kernel(tc, x, centres, sigmas, w1, b1, out):
                 for stage, lag in order:
                     if step >= lag:
                         stage(step - lag)
+                if step == 2:
+                    quantise_weights()
         finish()

import concourse.mybir as mybir
from concourse.masks import make_identity

F32 = mybir.dt.float32
BF16 = mybir.dt.bfloat16
U32 = mybir.dt.uint32
U8 = mybir.dt.uint8
FP8X4 = mybir.dt.float8_e4m3fn_x4
ALU = mybir.AluOpType
ACT = mybir.ActivationFunctionType
AXIS = mybir.AxisListType
ENGINE = mybir.EngineType

P = 128
PACK = 4
ROWS, IN, HID, CENT = 16384, 128, 512, 256
SUBS = 4
CHUNK = SUBS * P
N_CHUNKS = ROWS // CHUNK
LAST = N_CHUNKS - 1
ALL = slice(0, CHUNK)
HALVES = (slice(0, CHUNK // 2), slice(CHUNK // 2, CHUNK))
PAIRS = ((0, 1), (2, 3))
CHUNKS_PER_LOAD = 4
VECTOR_COPIES = 3
GPSIMD_FROM = 384
VECTOR_ROWS = GPSIMD_FROM + 8

FLOPS = 2 * ROWS * IN * HID + 2 * ROWS * HID * CENT


def tile_networkprc_pa_t_kernel(tc, x, centres, sigmas, w1, b1, out):
    nc = tc.nc
    assert HID == P * PACK and IN == P and CENT == 2 * P

    x_view = x.rearrange("(q p u) k -> p q (u k)", p=P, u=SUBS)
    out_view = out.rearrange("(q p u) c -> q p (u c)", p=P, u=SUBS)

    with tc.tile_pool(name="keep", bufs=1) as keep, tc.tile_pool(name="work", bufs=3) as work, tc.psum_pool(
        name="psum_xt", bufs=1
    ) as psum_xt, tc.psum_pool(name="psum_dist", bufs=4) as psum_dist, tc.psum_pool(
        name="psum_acc", bufs=3
    ) as psum_acc:
        x_all = keep.tile([P, N_CHUNKS, CHUNK], BF16)
        c_rows = keep.tile([P, PACK, IN], BF16)
        sig = keep.tile([P, PACK], BF16)
        w_rows = keep.tile([P, 2, HID], BF16)
        bias = keep.tile([P, CENT], BF16)

        def load_chunks(first, end):
            nc.sync.dma_start(out=x_all[:, first:end, :], in_=x_view[:, first:end, :])

        load_chunks(0, 1)
        nc.sync.dma_start(out=c_rows[:], in_=centres.rearrange("(p t) k -> p t k", t=PACK))
        nc.sync.dma_start(out=sig[:], in_=sigmas.rearrange("(p t) -> p t", t=PACK))
        load_chunks(1, 2)
        load_chunks(2, CHUNKS_PER_LOAD)
        nc.sync.dma_start(out=w_rows[:], in_=w1.rearrange("(b p) j -> p b j", p=P))
        nc.sync.dma_start(out=bias[:], in_=b1.partition_broadcast(P))
        for q in range(CHUNKS_PER_LOAD, N_CHUNKS, CHUNKS_PER_LOAD):
            load_chunks(q, q + CHUNKS_PER_LOAD)

        ident_bf = keep.tile([P, P], BF16)
        make_identity(nc, ident_bf[:])
        ident_f32 = keep.tile([P, P], F32)
        make_identity(nc, ident_f32[:])

        x_turned, x_cols, x_norm, phi, phi_grouped, phi_codes, phi_scales, sums, biased = {}, {}, {}, {}, {}, {}, {}, {}, {}

        def rows_of(q, u):
            return x_all[:, q, u * IN : (u + 1) * IN]

        def square_rows(q):
            squares = work.tile([P, SUBS, IN], BF16)
            norms = work.tile([P, SUBS], F32)
            for u in range(SUBS):
                nc.scalar.activation(
                    out=squares[:, u, :], in_=rows_of(q, u), func=ACT.Square, accum_out=norms[:, u : u + 1]
                )
            x_norm[q] = norms

        def transpose_rows(q):
            xt_ps = psum_xt.tile([P, SUBS, P], BF16)
            for u in range(SUBS):
                nc.tensor.transpose(out=xt_ps[:, u, :], in_=rows_of(q, u), identity=ident_bf[:])
            cols = work.tile([P, SUBS, P], BF16)
            x_cols[q] = cols
            x_turned[q] = xt_ps

        def copy_on_scalar(q):
            nc.scalar.copy(out=x_cols[q][:], in_=x_turned[q][:])

        def copy_on_vector(q):
            if q % VECTOR_COPIES == 0:
                nc.vector.tensor_copy(out=x_cols[q][:], in_=x_turned[q][:])

        def square_and_transpose(q):
            if q not in x_norm:
                square_rows(q)
            transpose_rows(q)
            if q % VECTOR_COPIES != 0:
                copy_on_scalar(q)

        c_cols = keep.tile([P, PACK, P], BF16)
        exp_scale = keep.tile([P, PACK], F32)
        exp_bias = keep.tile([P, PACK], F32)

        def prepare_centres():
            c_squares = keep.tile([P, PACK, IN], F32)
            nc.vector.tensor_tensor(out=c_squares[:], in0=c_rows[:], in1=c_rows[:], op=ALU.mult)
            ct_ps = psum_acc.tile([P, PACK, P], BF16, tag="acc")
            for t in range(PACK):
                nc.tensor.transpose(out=ct_ps[:, t, :], in_=c_rows[:, t, :], identity=ident_bf[:])
            nc.vector.tensor_scalar(out=c_cols[:], in0=ct_ps[:], scalar1=-2.0, scalar2=None, op0=ALU.mult)
            c_norm = keep.tile([P, PACK], F32)
            nc.vector.tensor_reduce(out=c_norm[:], in_=c_squares[:], axis=AXIS.X, op=ALU.add)
            nc.vector.scalar_tensor_tensor(
                out=exp_scale[:], in0=sig[:], scalar=-1.0, in1=sig[:], op0=ALU.mult, op1=ALU.mult
            )
            nc.vector.tensor_tensor(out=exp_bias[:], in0=exp_scale[:], in1=c_norm[:], op=ALU.mult)

        w_codes = keep.tile([P, CENT], U32, align_bytes=64)
        w_scales = keep.tile([P, CENT], U8, align_bytes=64)

        def quantise_weights():
            acc = psum_acc.tile([P, 2, CENT], F32)
            for b in range(2):
                words = w_rows[:, b, :].bitcast(F32).rearrange("c (p h) -> c h p", h=2)
                for h in range(2):
                    nc.tensor.transpose(out=acc[:, h, b * P : (b + 1) * P], in_=words[:, h, :], identity=ident_f32[:])
            w_grouped = keep.tile([P, CENT * PACK], BF16, align_bytes=64)
            nc.vector.tensor_copy(
                out=w_grouped[:].bitcast(F32).rearrange("p (c h) -> p c h", h=2), in_=acc[:].rearrange("p h c -> p c h")
            )
            nc.vector.quantize_mx(out=w_codes[:].bitcast(FP8X4), scales=w_scales[:], in_=w_grouped[:])

        def distances_with_norms(q, planes):
            banks = []
            for t in planes:
                dist = psum_dist.tile([P, CHUNK], F32)
                nc.tensor.matmul(
                    out=dist[:],
                    lhsT=c_cols[:, t, :],
                    rhs=x_cols[q][:].rearrange("k u p -> k (u p)"),
                    start=True,
                    stop=False,
                )
                banks.append((t, dist))
            for t, dist in banks:
                for u in range(SUBS):
                    nc.tensor.matmul(
                        out=dist[:, u * P : (u + 1) * P],
                        lhsT=x_norm[q][:, u : u + 1].to_broadcast([P, P]),
                        rhs=ident_f32[:],
                        is_transpose=True,
                        start=False,
                        stop=(u == SUBS - 1),
                    )
            return banks

        def exp(q, t, dist, rows=ALL):
            nc.scalar.activation(
                out=phi[q][:, t, rows],
                in_=dist[:, rows],
                func=ACT.Exp,
                scale=exp_scale[:, t : t + 1],
                bias=exp_bias[:, t : t + 1],
            )

        def new_phi(q):
            planes = work.tile([P, PACK, CHUNK], BF16)
            phi[q] = planes

        def exp_of_planes(q, planes):
            for t, dist in distances_with_norms(q, planes):
                exp(q, t, dist)

        def new_grouped(q):
            grouped = work.tile([P, CHUNK * PACK], BF16, align_bytes=64)
            phi_grouped[q] = grouped

        def regroup_on_gpsimd(q):
            nc.gpsimd.tensor_scalar(
                out=phi_grouped[q][:, GPSIMD_FROM * PACK :].rearrange("p (n t) -> p n t", t=PACK),
                in0=phi[q][:, :, GPSIMD_FROM:].rearrange("p t n -> p n t"),
                scalar1=1.0,
                scalar2=0.0,
                op0=ALU.min,
                op1=ALU.max,
            )

        def regroup(q, rows=slice(0, VECTOR_ROWS)):
            if rows.start == 0:
                new_grouped(q)
            words = slice(rows.start * PACK, rows.stop * PACK)
            nc.vector.tensor_scalar(
                out=phi_grouped[q][:, words].rearrange("p (c i t) -> p c t i", i=2, t=PACK),
                in0=phi[q][:, :, rows].rearrange("p t (c i) -> p c t i", i=2),
                scalar1=1.0,
                scalar2=None,
                op0=ALU.min,
            )

        def quantise(q, rows=ALL):
            if rows.start == 0:
                codes = work.tile([P, CHUNK], U32, align_bytes=64)
                scales = work.tile([P, CHUNK], U8, align_bytes=64)
                phi_codes[q], phi_scales[q] = codes, scales
            nc.vector.quantize_mx(
                out=phi_codes[q][:, rows].bitcast(FP8X4),
                scales=phi_scales[q][:, rows],
                in_=phi_grouped[q][:, rows.start * PACK : rows.stop * PACK],
            )

        def project_half(q, half):
            acc = psum_acc.tile([P, 2, CENT], F32)
            for v in range(2):
                n_cols = slice((2 * half + v) * P, (2 * half + v + 1) * P)
                nc.tensor.matmul_mx(
                    out=acc[:, v, :],
                    lhsT=phi_codes[q][:, n_cols].bitcast(FP8X4),
                    lhsT_scale=phi_scales[q][:, n_cols],
                    rhs=w_codes[:].bitcast(FP8X4),
                    rhs_scale=w_scales[:],
                    start=True,
                    stop=True,
                )
            sums[q, half] = acc

        def project(q):
            for half in range(2):
                project_half(q, half)

        def add_bias_half(q, half):
            if half == 0:
                result = work.tile([P, SUBS, CENT], F32, bufs=6)
                biased[q] = result
            nc.vector.tensor_tensor(
                out=biased[q][:, 2 * half : 2 * half + 2, :],
                in0=sums[q, half][:],
                in1=bias[:].unsqueeze(1).to_broadcast([P, 2, CENT]),
                op=ALU.add,
            )

        def add_bias(q):
            for half in range(2):
                add_bias_half(q, half)

        def relu(tile):
            nc.vector.tensor_scalar(out=tile, in0=tile, scalar1=0.0, scalar2=None, op0=ALU.max)

        def relu_on_scalar(tile):
            nc.scalar.activation(out=tile, in_=tile, func=ACT.Relu)

        def store(q, subs=slice(0, SUBS)):
            nc.sync.dma_start(
                out=out_view[q][:, subs.start * CENT : subs.stop * CENT],
                in_=biased[q][:, subs, :].rearrange("p u c -> p (u c)"),
            )

        def relu_and_store(q):
            relu(biased[q][:])
            store(q)

        def relu_on_scalar_and_store(q):
            relu_on_scalar(biased[q][:])
            store(q)

        def warm_up():
            zeros = keep.tile([P, P], BF16)
            nc.vector.memset(zeros[:], 0.0)
            acc = psum_acc.tile([P, CHUNK], F32)
            for i in range(12):
                nc.tensor.matmul(out=acc[:, 0:P], lhsT=zeros[:], rhs=zeros[:], start=True, stop=True)

        def start():
            with tc.manual_schedule(engines={ENGINE.PE, ENGINE.Activation, ENGINE.DVE}):
                warm_up()
                square_rows(0)
                transpose_rows(0)
                copy_on_scalar(0)
                prepare_centres()
                square_rows(1)
                square_rows(2)
                new_phi(0)
                exp_of_planes(0, (0,))
                exp_of_planes(0, (1,))
                transpose_rows(1)
                copy_on_scalar(1)
                exp_of_planes(0, PAIRS[1])

        def distances_and_exp(q):
            new_phi(q)
            for pair in PAIRS:
                exp_of_planes(q, pair)

        def add_bias_sub(q, sub):
            nc.vector.tensor_tensor(
                out=biased[q][:, sub, :], in0=sums[q, sub // 2][:, sub % 2, :], in1=bias[:], op=ALU.add
            )

        def finish():
            with tc.manual_schedule(engines={ENGINE.PE, ENGINE.Activation, ENGINE.DVE}):
                new_phi(LAST)
                banks = distances_with_norms(LAST, PAIRS[0]) + distances_with_norms(LAST, PAIRS[1])
                project(LAST - 2)
                for rows in HALVES:
                    for t, dist in banks:
                        exp(LAST, t, dist, rows)
                regroup(LAST - 1)
                regroup_on_gpsimd(LAST - 1)
                add_bias(LAST - 3)
                relu_on_scalar_and_store(LAST - 4)
                relu_on_scalar_and_store(LAST - 3)
                quantise(LAST - 1)
                project(LAST - 1)
                add_bias(LAST - 2)
                relu_on_scalar_and_store(LAST - 2)
                regroup(LAST, HALVES[0])
                regroup_on_gpsimd(LAST)
                add_bias_half(LAST - 1, 0)
                quantise(LAST, HALVES[0])
                project_half(LAST, 0)
                regroup(LAST, slice(HALVES[1].start, GPSIMD_FROM))
                add_bias_half(LAST - 1, 1)
                relu_on_scalar_and_store(LAST - 1)
                quantise(LAST, HALVES[1])
                project_half(LAST, 1)
                add_bias_half(LAST, 0)
                relu_on_scalar(biased[LAST][:, 0:2, :])
                store(LAST, slice(0, 2))
                for sub in (2, 3):
                    add_bias_sub(LAST, sub)
                for sub in (2, 3):
                    relu(biased[LAST][:, sub, :])
                    store(LAST, slice(sub, sub + 1))

        order = (
            (square_and_transpose, 0),
            (distances_and_exp, 1),
            (project, 3),
            (copy_on_vector, 0),
            (regroup, 2),
            (regroup_on_gpsimd, 2),
            (add_bias, 4),
            (relu_and_store, 5),
            (quantise, 2),
        )
        start()
        with tc.manual_schedule(engines={ENGINE.PE, ENGINE.Activation, ENGINE.DVE}):
            for step in range(2, N_CHUNKS):
                for stage, lag in order:
                    if step >= lag:
                        stage(step - lag)
                if step == 2:
                    quantise_weights()
        finish()
